import numpy as np
import ml_dtypes


def mxq(x, axis, fmt="e4m3"):
    dtype, down = {"e4m3": (ml_dtypes.float8_e4m3fn, 7), "e5m2": (ml_dtypes.float8_e5m2, 14)}[fmt]
    v = np.moveaxis(np.asarray(x, np.float32).astype(ml_dtypes.bfloat16).astype(np.float64), axis, -1)
    blocks = v.reshape(v.shape[:-1] + (-1, 32))
    amax = np.abs(blocks).max(-1, keepdims=True)
    byte = np.maximum(np.where(amax > 0, np.frexp(amax)[1] - 1 + 127, 0) - down, 1)
    scale = np.exp2(byte - 127.0)
    codes = (blocks / scale).astype(np.float32).astype(dtype).astype(np.float64)
    return np.moveaxis((codes * scale).reshape(v.shape), -1, axis)


WIDE = False


def mx_kscale(k):
    if not WIDE:
        return np.ones(k)
    levels = np.array([10, -10, 5, -5, 0])
    a = np.random.permutation(np.resize(levels, k // 512 * 4)).reshape(k // 512, 4)
    idx = np.arange(k)
    return np.exp2(a[idx // 512, idx % 128 // 32])


BF16 = ml_dtypes.bfloat16


def bf(x):
    return np.asarray(x, np.float32).astype(BF16)


def f64(x):
    return np.asarray(x).astype(np.float64)


B, C, H, D, N, CO = 16, 128, 2048, 512, 4, 128
NC = N * C
EPS = 1e-5


def bn(v, gamma, beta, axes):
    mean = v.mean(axis=axes, keepdims=True)
    var = v.var(axis=axes, keepdims=True)
    return (v - mean) / np.sqrt(var + EPS) * gamma + beta


def setup_inputs():
    u = mx_kscale(NC)
    head = np.maximum(np.random.standard_normal((N, B, C, D)), 0.0) + 0.25 * np.random.standard_normal((N, B, C, D))
    return {'head_res': bf(head * u.reshape(N, 1, C, 1)),
            'W_merge': bf(np.random.standard_normal((CO, NC)) / np.sqrt(NC) / u[None, :]),
            'g_m': bf(1.0 + 0.1 * np.random.standard_normal(CO)),
            'b_m': bf(0.1 * np.random.standard_normal(CO))}


def reference(head_res, W_merge, g_m, b_m):
    cat = f64(head_res).transpose(1, 0, 2, 3).reshape(B, NC, D)
    m = mxq(f64(W_merge), 1, 'e4m3')[None] @ mxq(cat, 1, 'e4m3')
    m = bn(m, f64(g_m)[None, :, None], f64(b_m)[None, :, None], (0, 2))
    return np.maximum(m, 0.0)

@@ -1,0 +1,219 @@
+from contextlib import ExitStack
+
+import concourse.mybir as mybir
+from concourse.masks import make_identity
+
+FLOPS = 2 * 16 * 128 * 512 * 512
+
+F32 = mybir.dt.float32
+BF16 = mybir.dt.bfloat16
+U32 = mybir.dt.uint32
+U8 = mybir.dt.uint8
+FP8X4 = mybir.dt.float8_e4m3fn_x4
+ALU = mybir.AluOpType
+ACT = mybir.ActivationFunctionType
+AX = mybir.AxisListType
+
+P = 128
+NH = 4
+NB = 16
+D = 512
+EPS = 1e-5
+CHUNKS = [1, 1, 2, 2, 2, 2, 2, 2, 1, 1]
+CV = 344
+MBUFS = 7
+MANUAL = True
+LAG_SWITCH = 8
+
+
+def tile_block_height_reducing_filtering_pb_t_kernel(tc, head_res, W_merge, g_m, b_m, out):
+    nc = tc.nc
+    with ExitStack() as ctx:
+        consts = ctx.enter_context(tc.tile_pool(name="consts", bufs=1))
+        rawp = ctx.enter_context(tc.tile_pool(name="rawp", bufs=1))
+        grpp = ctx.enter_context(tc.tile_pool(name="grpp", bufs=4))
+        codep = ctx.enter_context(tc.tile_pool(name="codep", bufs=1))
+        outp = ctx.enter_context(tc.tile_pool(name="outp", bufs=1))
+        small = ctx.enter_context(tc.tile_pool(name="small", bufs=1))
+        psum = ctx.enter_context(tc.psum_pool(name="psum", bufs=MBUFS))
+        if MANUAL:
+            ctx.enter_context(tc.manual_schedule())
+
+        w_sb = consts.tile([P, NH * P], BF16, name="w_sb")
+        nc.scalar.dma_start(out=w_sb[:], in_=W_merge)
+        g_bf = small.tile([P, 1], BF16, name="g_bf")
+        b_bf = small.tile([P, 1], BF16, name="b_bf")
+        with nc.allow_non_contiguous_dma(reason="one gain and one shift per partition, 128 elements each"):
+            nc.scalar.dma_start(out=g_bf[:], in_=g_m.rearrange("(o u) -> o u", u=1))
+            nc.scalar.dma_start(out=b_bf[:], in_=b_m.rearrange("(o u) -> o u", u=1))
+
+        raw_of = []
+        b0 = 0
+        for ci, nb in enumerate(CHUNKS):
+            raw = rawp.tile([P, nb, NH * D], BF16, name="raw%d" % ci)
+            for n in range(NH):
+                nc.sync.dma_start(
+                    out=raw[n:P:NH, :, :],
+                    in_=head_res[n, b0 : b0 + nb].rearrange("b (q t) d -> q b (t d)", t=4),
+                )
+            for j in range(nb):
+                raw_of.append((raw, j))
+            b0 += nb
+
+        one = small.tile([P, 1], F32, name="one")
+        nc.vector.memset(one[:], 1.0)
+        warm = small.tile([P, 1], F32, name="warm")
+        nc.scalar.activation(out=warm[:], in_=one[:], func=ACT.Sqrt)
+        ident = consts.tile([P, P], BF16, name="ident")
+        make_identity(nc, ident[:])
+
+        w_perm = consts.tile([P, 4, P], BF16, name="w_perm")
+        nc.vector.tensor_copy(
+            out=w_perm[:].rearrange("o t (q n) -> o t q n", n=NH),
+            in_=w_sb[:].rearrange("o (n q t) -> o t q n", n=NH, t=4),
+        )
+        wT_ps = psum.tile([P, 4, P], BF16, name="wT_ps", tag="m")
+        for t in range(4):
+            nc.tensor.transpose(wT_ps[:, t, :], w_perm[:, t, :], ident[:])
+        w_grp = consts.tile([P, P, 4], BF16, name="w_grp", align_bytes=64)
+        nc.scalar.copy(out=w_grp[:], in_=wT_ps[:].rearrange("p t o -> p o t"))
+        w_codes = consts.tile([P, P], U32, name="w_codes", align_bytes=64)
+        w_scales = consts.tile([P, P], U8, name="w_scales", align_bytes=64)
+
+        g32 = small.tile([P, 1], F32, name="g32")
+        b32 = small.tile([P, 1], F32, name="b32")
+
+        acc = psum.tile([P, D], F32, name="acc", tag="acc", bufs=1)
+        ss = small.tile([P, NB], F32, name="ss")
+        junk = consts.tile([P, D], F32, name="junk")
+        csum = small.tile([P, 1], F32, name="csum")
+        negc = small.tile([P, 1], F32, name="negc")
+
+        grp_of = {}
+        codes_of = {}
+        scales_of = {}
+        m_of = {}
+
+        def regroup(b):
+            raw, j = raw_of[b]
+            grp = grpp.tile([P, D, 4], BF16, name="grp", align_bytes=64)
+            grp_of[b] = grp
+            src = raw[:, j, :].rearrange("p (t d) -> p t d", t=4)
+            nc.vector.tensor_copy(
+                out=grp[:, 0:CV, :].rearrange("p (c i) t -> p c t i", i=4),
+                in_=src[:, :, 0:CV].rearrange("p t (c i) -> p c t i", i=4),
+            )
+            nc.scalar.copy(
+                out=grp[:, CV:D, :].rearrange("p (c i) t -> p c t i", i=4),
+                in_=src[:, :, CV:D].rearrange("p t (c i) -> p c t i", i=4),
+            )
+
+        def quantise(b):
+            codes = codep.tile([P, D], U32, name="codes%d" % b, align_bytes=64)
+            scales = codep.tile([P, D], U8, name="scales%d" % b, align_bytes=64)
+            codes_of[b] = codes
+            scales_of[b] = scales
+            nc.vector.quantize_mx(
+                out=codes[:].bitcast(FP8X4),
+                scales=scales[:],
+                in_=grp_of[b][:].rearrange("p d t -> p (d t)"),
+            )
+
+        def product(dst, b, start, stop):
+            nc.tensor.matmul_mx(
+                out=dst,
+                lhsT=w_codes[:].bitcast(FP8X4),
+                lhsT_scale=w_scales[:],
+                rhs=codes_of[b][:].bitcast(FP8X4),
+                rhs_scale=scales_of[b][:],
+                start=start,
+                stop=stop,
+            )
+
+        def multiply(b):
+            product(acc[:], b, b == 0, b == NB - 1)
+            m = psum.tile([P, D], F32, name="m%d" % b, tag="m")
+            m_of[b] = m
+            product(m[:], b, True, True)
+
+        def squares(b):
+            nc.scalar.activation(
+                out=junk[:], in_=m_of[b][:], func=ACT.Square, bias=negc[:, 0:1], scale=1.0,
+                accum_out=ss[:, b : b + 1],
+            )
+
+        sq_next = 0
+        for s in range(NB + 1):
+            if s < NB:
+                regroup(s)
+            if s == 1:
+                nc.vector.quantize_mx(
+                    out=w_codes[:].bitcast(FP8X4), scales=w_scales[:],
+                    in_=w_grp[:].rearrange("p o t -> p (o t)"),
+                )
+            if s == 2:
+                nc.vector.reduce_sum(out=csum[:], in_=m_of[0][:], axis=AX.X)
+                nc.vector.tensor_scalar(out=negc[:], in0=csum[:], scalar1=-1.0 / D, scalar2=None, op0=ALU.mult)
+                nc.vector.tensor_copy(out=g32[:], in_=g_bf[:])
+                nc.vector.tensor_copy(out=b32[:], in_=b_bf[:])
+            if s >= 1:
+                quantise(s - 1)
+                multiply(s - 1)
+            lag = 3 if s < LAG_SWITCH else 2
+            while sq_next <= s - lag:
+                squares(sq_next)
+                sq_next += 1
+        inv = 1.0 / (NB * D)
+        ssp = small.tile([P, 1], F32, name="ssp")
+        bias2 = small.tile([P, 1], F32, name="bias2")
+        bias2b = small.tile([P, 1], F32, name="bias2b")
+        s1 = small.tile([P, 1], F32, name="s1")
+        dpos = small.tile([P, 1], F32, name="dpos")
+        dneg = small.tile([P, 1], F32, name="dneg")
+        nmean = small.tile([P, 1], F32, name="nmean")
+        ngm = small.tile([P, 1], F32, name="ngm")
+        bias3 = small.tile([P, 1], F32, name="bias3")
+        std = small.tile([P, 1], F32, name="std")
+        rstd = small.tile([P, 1], F32, name="rstd")
+        gain = small.tile([P, 1], F32, name="gain")
+        shift = small.tile([P, 1], F32, name="shift")
+        nc.vector.reduce_sum(out=ssp[:], in_=ss[:, 0 : NB - 2], axis=AX.X)
+        nc.vector.tensor_scalar(out=bias2[:], in0=ssp[:], scalar1=inv, scalar2=EPS, op0=ALU.mult, op1=ALU.add)
+        squares(NB - 1)
+        nc.vector.reduce_sum(out=s1[:], in_=acc[:], axis=AX.X)
+        nc.vector.tensor_scalar(out=dpos[:], in0=s1[:], scalar1=inv, scalar2=negc[:, 0:1], op0=ALU.mult, op1=ALU.add)
+        nc.vector.tensor_scalar(
+            out=dneg[:], in0=s1[:], scalar1=-inv, scalar2=negc[:, 0:1], op0=ALU.mult, op1=ALU.subtract
+        )
+        nc.vector.scalar_tensor_tensor(
+            out=bias2b[:], in0=ss[:, NB - 2 : NB - 1], scalar=inv, in1=bias2[:], op0=ALU.mult, op1=ALU.add
+        )
+        nc.vector.scalar_tensor_tensor(
+            out=bias3[:], in0=dpos[:], scalar=dneg[:, 0:1], in1=bias2b[:], op0=ALU.mult, op1=ALU.add
+        )
+        nc.scalar.activation(out=std[:], in_=ss[:, NB - 1 : NB], func=ACT.Sqrt, bias=bias3[:, 0:1], scale=inv)
+        nc.vector.tensor_scalar(out=nmean[:], in0=s1[:], scalar1=-inv, scalar2=None, op0=ALU.mult)
+        nc.vector.tensor_tensor(out=ngm[:], in0=nmean[:], in1=g32[:], op=ALU.mult)
+        nc.vector.reciprocal(out=rstd[:], in_=std[:])
+        nc.vector.tensor_tensor(out=gain[:], in0=g32[:], in1=rstd[:], op=ALU.mult)
+        nc.vector.scalar_tensor_tensor(
+            out=shift[:], in0=ngm[:], scalar=rstd[:, 0:1], in1=b32[:], op0=ALU.mult, op1=ALU.add
+        )
+
+        first_kept = NB - MBUFS
+        order = list(range(first_kept, NB)) + list(range(0, first_kept))
+        for i, b in enumerate(order):
+            if b < first_kept:
+                m = psum.tile([P, D], F32, name="r%d" % b, tag="m")
+                product(m[:], b, True, True)
+            else:
+                m = m_of[b]
+            o = outp.tile([P, D], F32, name="o%d" % b)
+            if i % 2 == 0:
+                nc.scalar.activation(out=o[:], in_=m[:], func=ACT.Relu, bias=shift[:, 0:1], scale=gain[:, 0:1])
+            else:
+                nc.vector.tensor_scalar(
+                    out=o[:], in0=m[:], scalar1=gain[:, 0:1], scalar2=shift[:, 0:1], op0=ALU.mult, op1=ALU.add
+                )
+                nc.vector.tensor_scalar_max(out=o[:], in0=o[:], scalar1=0.0)
+            nc.sync.dma_start(out=out[b], in_=o[:])

@@ -19,11 +19,14 @@ NH = 4
 NB = 16
 D = 512
 EPS = 1e-5
-CHUNKS = [1, 1, 2, 2, 2, 2, 2, 2, 1, 1]
-CV = 344
+CHUNKS = [1, 1, 1, 1, 1, 1, 1, 1, 2, 2, 2, 2]
+CV = 352
+CV_LAST = 400
 MBUFS = 7
+HALF = 256
+PIV = 64
 MANUAL = True
-LAG_SWITCH = 8
+LAG_SWITCH = 99
 
 
 def tile_block_height_reducing_filtering_pb_t_kernel(tc, head_res, W_merge, g_m, b_m, out):
@@ -51,11 +54,19 @@ def tile_block_height_reducing_filtering_pb_t_kernel(tc, head_res, W_merge, g_m,
         b0 = 0
         for ci, nb in enumerate(CHUNKS):
             raw = rawp.tile([P, nb, NH * D], BF16, name="raw%d" % ci)
-            for n in range(NH):
-                nc.sync.dma_start(
-                    out=raw[n:P:NH, :, :],
-                    in_=head_res[n, b0 : b0 + nb].rearrange("b (q t) d -> q b (t d)", t=4),
-                )
+            if ci == 0:
+                for h in range(2):
+                    for n in range(NH):
+                        nc.sync.dma_start(
+                            out=raw[n:P:NH, 0, :].rearrange("q (t d) -> q t d", t=4)[:, :, h * HALF : (h + 1) * HALF],
+                            in_=head_res[n, 0, :, h * HALF : (h + 1) * HALF].rearrange("(q t) d -> q t d", t=4),
+                        )
+            else:
+                for n in range(NH):
+                    nc.sync.dma_start(
+                        out=raw[n:P:NH, :, :],
+                        in_=head_res[n, b0 : b0 + nb].rearrange("b (q t) d -> q b (t d)", t=4),
+                    )
             for j in range(nb):
                 raw_of.append((raw, j))
             b0 += nb
@@ -76,7 +87,6 @@ def tile_block_height_reducing_filtering_pb_t_kernel(tc, head_res, W_merge, g_m,
         for t in range(4):
             nc.tensor.transpose(wT_ps[:, t, :], w_perm[:, t, :], ident[:])
         w_grp = consts.tile([P, P, 4], BF16, name="w_grp", align_bytes=64)
-        nc.scalar.copy(out=w_grp[:], in_=wT_ps[:].rearrange("p t o -> p o t"))
         w_codes = consts.tile([P, P], U32, name="w_codes", align_bytes=64)
         w_scales = consts.tile([P, P], U8, name="w_scales", align_bytes=64)
 
@@ -86,7 +96,6 @@ def tile_block_height_reducing_filtering_pb_t_kernel(tc, head_res, W_merge, g_m,
         acc = psum.tile([P, D], F32, name="acc", tag="acc", bufs=1)
         ss = small.tile([P, NB], F32, name="ss")
         junk = consts.tile([P, D], F32, name="junk")
-        csum = small.tile([P, 1], F32, name="csum")
         negc = small.tile([P, 1], F32, name="negc")
 
         grp_of = {}
@@ -94,19 +103,28 @@ def tile_block_height_reducing_filtering_pb_t_kernel(tc, head_res, W_merge, g_m,
         scales_of = {}
         m_of = {}
 
-        def regroup(b):
+        def regroup_part(b, d0, d1):
             raw, j = raw_of[b]
-            grp = grpp.tile([P, D, 4], BF16, name="grp", align_bytes=64)
-            grp_of[b] = grp
+            grp = grp_of[b]
             src = raw[:, j, :].rearrange("p (t d) -> p t d", t=4)
+            dv = d0 + (d1 - d0) * (CV if b < NB - 3 else CV_LAST) // D
             nc.vector.tensor_copy(
-                out=grp[:, 0:CV, :].rearrange("p (c i) t -> p c t i", i=4),
-                in_=src[:, :, 0:CV].rearrange("p t (c i) -> p c t i", i=4),
+                out=grp[:, d0:dv, :].rearrange("p (c i) t -> p c t i", i=4),
+                in_=src[:, :, d0:dv].rearrange("p t (c i) -> p c t i", i=4),
             )
             nc.scalar.copy(
-                out=grp[:, CV:D, :].rearrange("p (c i) t -> p c t i", i=4),
-                in_=src[:, :, CV:D].rearrange("p t (c i) -> p c t i", i=4),
+                out=grp[:, dv:d1, :].rearrange("p (c i) t -> p c t i", i=4),
+                in_=src[:, :, dv:d1].rearrange("p t (c i) -> p c t i", i=4),
             )
+
+        def regroup(b):
+            grp = grpp.tile([P, D, 4], BF16, name="grp", align_bytes=64)
+            grp_of[b] = grp
+            if b == 0:
+                regroup_part(b, 0, HALF)
+                regroup_part(b, HALF, D)
+            else:
+                regroup_part(b, 0, D)
 
         def quantise(b):
             codes = codep.tile([P, D], U32, name="codes%d" % b, align_bytes=64)
@@ -146,19 +164,23 @@ def tile_block_height_reducing_filtering_pb_t_kernel(tc, head_res, W_merge, g_m,
         for s in range(NB + 1):
             if s < NB:
                 regroup(s)
+            if s == 0:
+                nc.scalar.copy(out=w_grp[:], in_=wT_ps[:].rearrange("p t o -> p o t"))
             if s == 1:
                 nc.vector.quantize_mx(
                     out=w_codes[:].bitcast(FP8X4), scales=w_scales[:],
                     in_=w_grp[:].rearrange("p o t -> p (o t)"),
                 )
-            if s == 2:
-                nc.vector.reduce_sum(out=csum[:], in_=m_of[0][:], axis=AX.X)
-                nc.vector.tensor_scalar(out=negc[:], in0=csum[:], scalar1=-1.0 / D, scalar2=None, op0=ALU.mult)
-                nc.vector.tensor_copy(out=g32[:], in_=g_bf[:])
-                nc.vector.tensor_copy(out=b32[:], in_=b_bf[:])
             if s >= 1:
                 quantise(s - 1)
                 multiply(s - 1)
+            if s == 2:
+                nc.scalar.activation(
+                    out=junk[:, 0:PIV], in_=m_of[0][:, 0:PIV], func=ACT.Identity, scale=-1.0 / PIV, accum_out=negc[:]
+                )
+            if s == 8:
+                nc.vector.tensor_copy(out=g32[:], in_=g_bf[:])
+                nc.vector.tensor_copy(out=b32[:], in_=b_bf[:])
             lag = 3 if s < LAG_SWITCH else 2
             while sq_next <= s - lag:
                 squares(sq_next)
@@ -179,7 +201,9 @@ def tile_block_height_reducing_filtering_pb_t_kernel(tc, head_res, W_merge, g_m,
         shift = small.tile([P, 1], F32, name="shift")
         nc.vector.reduce_sum(out=ssp[:], in_=ss[:, 0 : NB - 2], axis=AX.X)
         nc.vector.tensor_scalar(out=bias2[:], in0=ssp[:], scalar1=inv, scalar2=EPS, op0=ALU.mult, op1=ALU.add)
-        squares(NB - 1)
+        while sq_next < NB:
+            squares(sq_next)
+            sq_next += 1
         nc.vector.reduce_sum(out=s1[:], in_=acc[:], axis=AX.X)
         nc.vector.tensor_scalar(out=dpos[:], in0=s1[:], scalar1=inv, scalar2=negc[:, 0:1], op0=ALU.mult, op1=ALU.add)
         nc.vector.tensor_scalar(
@@ -200,16 +224,12 @@ def tile_block_height_reducing_filtering_pb_t_kernel(tc, head_res, W_merge, g_m,
             out=shift[:], in0=ngm[:], scalar=rstd[:, 0:1], in1=b32[:], op0=ALU.mult, op1=ALU.add
         )
 
-        first_kept = NB - MBUFS
-        order = list(range(first_kept, NB)) + list(range(0, first_kept))
-        for i, b in enumerate(order):
-            if b < first_kept:
-                m = psum.tile([P, D], F32, name="r%d" % b, tag="m")
-                product(m[:], b, True, True)
-            else:
-                m = m_of[b]
+        for b in range(NB):
+            i = b
+            m = psum.tile([P, D], F32, name="r%d" % b, tag="m")
+            product(m[:], b, True, True)
             o = outp.tile([P, D], F32, name="o%d" % b)
-            if i % 2 == 0:
+            if i % 3 != 1:
                 nc.scalar.activation(out=o[:], in_=m[:], func=ACT.Relu, bias=shift[:, 0:1], scale=gain[:, 0:1])
             else:
                 nc.vector.tensor_scalar(

@@ -74,7 +74,7 @@ def tile_block_height_reducing_filtering_pb_t_kernel(tc, head_res, W_merge, g_m,
         one = small.tile([P, 1], F32, name="one")
         nc.vector.memset(one[:], 1.0)
         warm = small.tile([P, 1], F32, name="warm")
-        nc.scalar.activation(out=warm[:], in_=one[:], func=ACT.Sqrt)
+        nc.scalar.activation(out=warm[:], in_=one[:], func=ACT.Abs_reciprocal_sqrt)
         ident = consts.tile([P, P], BF16, name="ident")
         make_identity(nc, ident[:])
 
@@ -195,7 +195,6 @@ def tile_block_height_reducing_filtering_pb_t_kernel(tc, head_res, W_merge, g_m,
         nmean = small.tile([P, 1], F32, name="nmean")
         ngm = small.tile([P, 1], F32, name="ngm")
         bias3 = small.tile([P, 1], F32, name="bias3")
-        std = small.tile([P, 1], F32, name="std")
         rstd = small.tile([P, 1], F32, name="rstd")
         gain = small.tile([P, 1], F32, name="gain")
         shift = small.tile([P, 1], F32, name="shift")
@@ -215,10 +214,11 @@ def tile_block_height_reducing_filtering_pb_t_kernel(tc, head_res, W_merge, g_m,
         nc.vector.scalar_tensor_tensor(
             out=bias3[:], in0=dpos[:], scalar=dneg[:, 0:1], in1=bias2b[:], op0=ALU.mult, op1=ALU.add
         )
-        nc.scalar.activation(out=std[:], in_=ss[:, NB - 1 : NB], func=ACT.Sqrt, bias=bias3[:, 0:1], scale=inv)
+        nc.scalar.activation(
+            out=rstd[:], in_=ss[:, NB - 1 : NB], func=ACT.Abs_reciprocal_sqrt, bias=bias3[:, 0:1], scale=inv
+        )
         nc.vector.tensor_scalar(out=nmean[:], in0=s1[:], scalar1=-inv, scalar2=None, op0=ALU.mult)
         nc.vector.tensor_tensor(out=ngm[:], in0=nmean[:], in1=g32[:], op=ALU.mult)
-        nc.vector.reciprocal(out=rstd[:], in_=std[:])
         nc.vector.tensor_tensor(out=gain[:], in0=g32[:], in1=rstd[:], op=ALU.mult)
         nc.vector.scalar_tensor_tensor(
             out=shift[:], in0=ngm[:], scalar=rstd[:, 0:1], in1=b32[:], op0=ALU.mult, op1=ALU.add
@@ -229,6 +229,14 @@ def tile_block_height_reducing_filtering_pb_t_kernel(tc, head_res, W_merge, g_m,
             m = psum.tile([P, D], F32, name="r%d" % b, tag="m")
             product(m[:], b, True, True)
             o = outp.tile([P, D], F32, name="o%d" % b)
+            if b == 0:
+                for h in range(2):
+                    cols = slice(h * HALF, (h + 1) * HALF)
+                    nc.scalar.activation(
+                        out=o[:, cols], in_=m[:, cols], func=ACT.Relu, bias=shift[:, 0:1], scale=gain[:, 0:1]
+                    )
+                    nc.sync.dma_start(out=out[b, :, cols], in_=o[:, cols])
+                continue
             if i % 3 != 1:
                 nc.scalar.activation(out=o[:], in_=m[:], func=ACT.Relu, bias=shift[:, 0:1], scale=gain[:, 0:1])
             else:

@@ -19,7 +19,7 @@ NH = 4
 NB = 16
 D = 512
 EPS = 1e-5
-CHUNKS = [1, 1, 1, 1, 1, 1, 1, 1, 2, 2, 2, 2]
+CHUNKS = [1] * 16
 CV = 352
 CV_LAST = 400
 MBUFS = 7
@@ -46,26 +46,16 @@ def tile_block_height_reducing_filtering_pb_t_kernel(tc, head_res, W_merge, g_m,
         nc.scalar.dma_start(out=w_sb[:], in_=W_merge)
         g_bf = small.tile([P, 1], BF16, name="g_bf")
         b_bf = small.tile([P, 1], BF16, name="b_bf")
-        with nc.allow_non_contiguous_dma(reason="one gain and one shift per partition, 128 elements each"):
-            nc.scalar.dma_start(out=g_bf[:], in_=g_m.rearrange("(o u) -> o u", u=1))
-            nc.scalar.dma_start(out=b_bf[:], in_=b_m.rearrange("(o u) -> o u", u=1))
 
         raw_of = []
         b0 = 0
         for ci, nb in enumerate(CHUNKS):
             raw = rawp.tile([P, nb, NH * D], BF16, name="raw%d" % ci)
-            if ci == 0:
-                for h in range(2):
-                    for n in range(NH):
-                        nc.sync.dma_start(
-                            out=raw[n:P:NH, 0, :].rearrange("q (t d) -> q t d", t=4)[:, :, h * HALF : (h + 1) * HALF],
-                            in_=head_res[n, 0, :, h * HALF : (h + 1) * HALF].rearrange("(q t) d -> q t d", t=4),
-                        )
-            else:
-                for n in range(NH):
+            for j in range(nb):
+                for a in range(2):
                     nc.sync.dma_start(
-                        out=raw[n:P:NH, :, :],
-                        in_=head_res[n, b0 : b0 + nb].rearrange("b (q t) d -> q b (t d)", t=4),
+                        out=raw[a:P:2, j, :].rearrange("c (b f) -> c b f", b=2),
+                        in_=head_res[2 * a : 2 * a + 2, b0 + j].rearrange("b (c e) d -> c b (e d)", e=2),
                     )
             for j in range(nb):
                 raw_of.append((raw, j))
@@ -79,10 +69,12 @@ def tile_block_height_reducing_filtering_pb_t_kernel(tc, head_res, W_merge, g_m,
         make_identity(nc, ident[:])
 
         w_perm = consts.tile([P, 4, P], BF16, name="w_perm")
-        nc.vector.tensor_copy(
-            out=w_perm[:].rearrange("o t (q n) -> o t q n", n=NH),
-            in_=w_sb[:].rearrange("o (n q t) -> o t q n", n=NH, t=4),
-        )
+        w_src = w_sb[:].rearrange("o (a b c e) -> o b e c a", a=2, b=2, e=2)
+        for b in range(2):
+            nc.vector.tensor_copy(
+                out=w_perm[:, 2 * b : 2 * b + 2, :].rearrange("o e (c a) -> o e c a", a=2),
+                in_=w_src[:, b],
+            )
         wT_ps = psum.tile([P, 4, P], BF16, name="wT_ps", tag="m")
         for t in range(4):
             nc.tensor.transpose(wT_ps[:, t, :], w_perm[:, t, :], ident[:])
@@ -120,11 +112,7 @@ def tile_block_height_reducing_filtering_pb_t_kernel(tc, head_res, W_merge, g_m,
         def regroup(b):
             grp = grpp.tile([P, D, 4], BF16, name="grp", align_bytes=64)
             grp_of[b] = grp
-            if b == 0:
-                regroup_part(b, 0, HALF)
-                regroup_part(b, HALF, D)
-            else:
-                regroup_part(b, 0, D)
+            regroup_part(b, 0, D)
 
         def quantise(b):
             codes = codep.tile([P, D], U32, name="codes%d" % b, align_bytes=64)
@@ -178,9 +166,10 @@ def tile_block_height_reducing_filtering_pb_t_kernel(tc, head_res, W_merge, g_m,
                 nc.scalar.activation(
                     out=junk[:, 0:PIV], in_=m_of[0][:, 0:PIV], func=ACT.Identity, scale=-1.0 / PIV, accum_out=negc[:]
                 )
-            if s == 8:
-                nc.vector.tensor_copy(out=g32[:], in_=g_bf[:])
-                nc.vector.tensor_copy(out=b32[:], in_=b_bf[:])
+            if s == 12:
+                with nc.allow_non_contiguous_dma(reason="one gain and one shift per partition, 128 elements each"):
+                    nc.scalar.dma_start(out=g_bf[:], in_=g_m.rearrange("(o u) -> o u", u=1))
+                    nc.scalar.dma_start(out=b_bf[:], in_=b_m.rearrange("(o u) -> o u", u=1))
             lag = 3 if s < LAG_SWITCH else 2
             while sq_next <= s - lag:
                 squares(sq_next)
@@ -198,6 +187,8 @@ def tile_block_height_reducing_filtering_pb_t_kernel(tc, head_res, W_merge, g_m,
         rstd = small.tile([P, 1], F32, name="rstd")
         gain = small.tile([P, 1], F32, name="gain")
         shift = small.tile([P, 1], F32, name="shift")
+        nc.vector.tensor_copy(out=g32[:], in_=g_bf[:])
+        nc.vector.tensor_copy(out=b32[:], in_=b_bf[:])
         nc.vector.reduce_sum(out=ssp[:], in_=ss[:, 0 : NB - 2], axis=AX.X)
         nc.vector.tensor_scalar(out=bias2[:], in0=ssp[:], scalar1=inv, scalar2=EPS, op0=ALU.mult, op1=ALU.add)
         while sq_next < NB:

@@ -20,8 +20,8 @@ NB = 16
 D = 512
 EPS = 1e-5
 CHUNKS = [1] * 16
-CV = 352
-CV_LAST = 400
+CV = 336
+CV_LAST = 384
 MBUFS = 7
 HALF = 256
 PIV = 64

@@ -19,14 +19,13 @@ NH = 4
 NB = 16
 D = 512
 EPS = 1e-5
-CHUNKS = [1] * 16
+UNITS = [1, 1, 2, 2, 2, 2, 2, 2, 1, 1]
 CV = 336
 CV_LAST = 384
 MBUFS = 7
 HALF = 256
 PIV = 64
-MANUAL = True
-LAG_SWITCH = 99
+LAGU = 2
 
 
 def tile_block_height_reducing_filtering_pb_t_kernel(tc, head_res, W_merge, g_m, b_m, out):
@@ -39,27 +38,28 @@ def tile_block_height_reducing_filtering_pb_t_kernel(tc, head_res, W_merge, g_m,
         outp = ctx.enter_context(tc.tile_pool(name="outp", bufs=1))
         small = ctx.enter_context(tc.tile_pool(name="small", bufs=1))
         psum = ctx.enter_context(tc.psum_pool(name="psum", bufs=MBUFS))
-        if MANUAL:
-            ctx.enter_context(tc.manual_schedule())
+        ctx.enter_context(tc.manual_schedule())
 
         w_sb = consts.tile([P, NH * P], BF16, name="w_sb")
         nc.scalar.dma_start(out=w_sb[:], in_=W_merge)
         g_bf = small.tile([P, 1], BF16, name="g_bf")
         b_bf = small.tile([P, 1], BF16, name="b_bf")
 
+        first_of = []
         raw_of = []
         b0 = 0
-        for ci, nb in enumerate(CHUNKS):
-            raw = rawp.tile([P, nb, NH * D], BF16, name="raw%d" % ci)
+        for u, nb in enumerate(UNITS):
+            raw = rawp.tile([P, nb, NH * D], BF16, name="raw%d" % u)
             for j in range(nb):
                 for a in range(2):
                     nc.sync.dma_start(
                         out=raw[a:P:2, j, :].rearrange("c (b f) -> c b f", b=2),
                         in_=head_res[2 * a : 2 * a + 2, b0 + j].rearrange("b (c e) d -> c b (e d)", e=2),
                     )
-            for j in range(nb):
-                raw_of.append((raw, j))
+            raw_of.append(raw)
+            first_of.append(b0)
             b0 += nb
+        NU = len(UNITS)
 
         one = small.tile([P, 1], F32, name="one")
         nc.vector.memset(one[:], 1.0)
@@ -95,43 +95,43 @@ def tile_block_height_reducing_filtering_pb_t_kernel(tc, head_res, W_merge, g_m,
         scales_of = {}
         m_of = {}
 
-        def regroup_part(b, d0, d1):
-            raw, j = raw_of[b]
-            grp = grp_of[b]
-            src = raw[:, j, :].rearrange("p (t d) -> p t d", t=4)
-            dv = d0 + (d1 - d0) * (CV if b < NB - 3 else CV_LAST) // D
+        def regroup(u):
+            nb = UNITS[u]
+            raw = raw_of[u]
+            grp = grpp.tile([P, nb, D, 4], BF16, name="grp", align_bytes=64)
+            grp_of[u] = grp
+            dv = CV if u < NU - 2 else CV_LAST
+            src = raw[:].rearrange("p j (t d) -> p j t d", t=4)
             nc.vector.tensor_copy(
-                out=grp[:, d0:dv, :].rearrange("p (c i) t -> p c t i", i=4),
-                in_=src[:, :, d0:dv].rearrange("p t (c i) -> p c t i", i=4),
+                out=grp[:, :, 0:dv, :].rearrange("p j (c i) t -> p j c t i", i=4),
+                in_=src[:, :, :, 0:dv].rearrange("p j t (c i) -> p j c t i", i=4),
             )
-            nc.scalar.copy(
-                out=grp[:, dv:d1, :].rearrange("p (c i) t -> p c t i", i=4),
-                in_=src[:, :, dv:d1].rearrange("p t (c i) -> p c t i", i=4),
-            )
+            for j in range(nb):
+                nc.scalar.copy(
+                    out=grp[:, j, dv:D, :].rearrange("p (c i) t -> p c t i", i=4),
+                    in_=src[:, j, :, dv:D].rearrange("p t (c i) -> p c t i", i=4),
+                )
 
-        def regroup(b):
-            grp = grpp.tile([P, D, 4], BF16, name="grp", align_bytes=64)
-            grp_of[b] = grp
-            regroup_part(b, 0, D)
-
-        def quantise(b):
-            codes = codep.tile([P, D], U32, name="codes%d" % b, align_bytes=64)
-            scales = codep.tile([P, D], U8, name="scales%d" % b, align_bytes=64)
-            codes_of[b] = codes
-            scales_of[b] = scales
+        def quantise(u):
+            nb = UNITS[u]
+            codes = codep.tile([P, nb * D], U32, name="codes%d" % u, align_bytes=64)
+            scales = codep.tile([P, nb * D], U8, name="scales%d" % u, align_bytes=64)
             nc.vector.quantize_mx(
                 out=codes[:].bitcast(FP8X4),
                 scales=scales[:],
-                in_=grp_of[b][:].rearrange("p d t -> p (d t)"),
+                in_=grp_of[u][:].rearrange("p j d t -> p (j d t)"),
             )
+            for j in range(nb):
+                codes_of[first_of[u] + j] = codes[:, j * D : (j + 1) * D]
+                scales_of[first_of[u] + j] = scales[:, j * D : (j + 1) * D]
 
         def product(dst, b, start, stop):
             nc.tensor.matmul_mx(
                 out=dst,
                 lhsT=w_codes[:].bitcast(FP8X4),
                 lhsT_scale=w_scales[:],
-                rhs=codes_of[b][:].bitcast(FP8X4),
-                rhs_scale=scales_of[b][:],
+                rhs=codes_of[b].bitcast(FP8X4),
+                rhs_scale=scales_of[b],
                 start=start,
                 stop=stop,
             )
@@ -149,31 +149,33 @@ def tile_block_height_reducing_filtering_pb_t_kernel(tc, head_res, W_merge, g_m,
             )
 
         sq_next = 0
-        for s in range(NB + 1):
-            if s < NB:
-                regroup(s)
-            if s == 0:
+        for u in range(NU + 1):
+            if u < NU:
+                regroup(u)
+            if u == 0:
                 nc.scalar.copy(out=w_grp[:], in_=wT_ps[:].rearrange("p t o -> p o t"))
-            if s == 1:
+            if u == 1:
                 nc.vector.quantize_mx(
                     out=w_codes[:].bitcast(FP8X4), scales=w_scales[:],
                     in_=w_grp[:].rearrange("p o t -> p (o t)"),
                 )
-            if s >= 1:
-                quantise(s - 1)
-                multiply(s - 1)
-            if s == 2:
+            if u >= 1:
+                quantise(u - 1)
+                for j in range(UNITS[u - 1]):
+                    multiply(first_of[u - 1] + j)
+            if u == 2:
                 nc.scalar.activation(
                     out=junk[:, 0:PIV], in_=m_of[0][:, 0:PIV], func=ACT.Identity, scale=-1.0 / PIV, accum_out=negc[:]
                 )
-            if s == 12:
+            if u == NU - 3:
                 with nc.allow_non_contiguous_dma(reason="one gain and one shift per partition, 128 elements each"):
                     nc.scalar.dma_start(out=g_bf[:], in_=g_m.rearrange("(o u) -> o u", u=1))
                     nc.scalar.dma_start(out=b_bf[:], in_=b_m.rearrange("(o u) -> o u", u=1))
-            lag = 3 if s < LAG_SWITCH else 2
-            while sq_next <= s - lag:
-                squares(sq_next)
-                sq_next += 1
+            if u >= 2 and u - LAGU < NU - 2:
+                while sq_next < first_of[u - LAGU] + UNITS[u - LAGU]:
+                    squares(sq_next)
+                    sq_next += 1
+
         inv = 1.0 / (NB * D)
         ssp = small.tile([P, 1], F32, name="ssp")
         bias2 = small.tile([P, 1], F32, name="bias2")
@@ -216,7 +218,6 @@ def tile_block_height_reducing_filtering_pb_t_kernel(tc, head_res, W_merge, g_m,
         )
 
         for b in range(NB):
-            i = b
             m = psum.tile([P, D], F32, name="r%d" % b, tag="m")
             product(m[:], b, True, True)
             o = outp.tile([P, D], F32, name="o%d" % b)
@@ -228,7 +229,7 @@ def tile_block_height_reducing_filtering_pb_t_kernel(tc, head_res, W_merge, g_m,
                     )
                     nc.sync.dma_start(out=out[b, :, cols], in_=o[:, cols])
                 continue
-            if i % 3 != 1:
+            if b % 3 != 1:
                 nc.scalar.activation(out=o[:], in_=m[:], func=ACT.Relu, bias=shift[:, 0:1], scale=gain[:, 0:1])
             else:
                 nc.vector.tensor_scalar(

@@ -19,13 +19,14 @@ NH = 4
 NB = 16
 D = 512
 EPS = 1e-5
-UNITS = [1, 1, 2, 2, 2, 2, 2, 2, 1, 1]
-CV = 336
-CV_LAST = 384
+CHUNKS = [1] * 16
+CV = 320
+CV_LAST = 368
 MBUFS = 7
 HALF = 256
 PIV = 64
-LAGU = 2
+MANUAL = True
+LAG_SWITCH = 99
 
 
 def tile_block_height_reducing_filtering_pb_t_kernel(tc, head_res, W_merge, g_m, b_m, out):
@@ -38,28 +39,27 @@ def tile_block_height_reducing_filtering_pb_t_kernel(tc, head_res, W_merge, g_m,
         outp = ctx.enter_context(tc.tile_pool(name="outp", bufs=1))
         small = ctx.enter_context(tc.tile_pool(name="small", bufs=1))
         psum = ctx.enter_context(tc.psum_pool(name="psum", bufs=MBUFS))
-        ctx.enter_context(tc.manual_schedule())
+        if MANUAL:
+            ctx.enter_context(tc.manual_schedule())
 
         w_sb = consts.tile([P, NH * P], BF16, name="w_sb")
         nc.scalar.dma_start(out=w_sb[:], in_=W_merge)
         g_bf = small.tile([P, 1], BF16, name="g_bf")
         b_bf = small.tile([P, 1], BF16, name="b_bf")
 
-        first_of = []
         raw_of = []
         b0 = 0
-        for u, nb in enumerate(UNITS):
-            raw = rawp.tile([P, nb, NH * D], BF16, name="raw%d" % u)
+        for ci, nb in enumerate(CHUNKS):
+            raw = rawp.tile([P, nb, NH * D], BF16, name="raw%d" % ci)
             for j in range(nb):
                 for a in range(2):
                     nc.sync.dma_start(
                         out=raw[a:P:2, j, :].rearrange("c (b f) -> c b f", b=2),
                         in_=head_res[2 * a : 2 * a + 2, b0 + j].rearrange("b (c e) d -> c b (e d)", e=2),
                     )
-            raw_of.append(raw)
-            first_of.append(b0)
+            for j in range(nb):
+                raw_of.append((raw, j))
             b0 += nb
-        NU = len(UNITS)
 
         one = small.tile([P, 1], F32, name="one")
         nc.vector.memset(one[:], 1.0)
@@ -95,43 +95,43 @@ def tile_block_height_reducing_filtering_pb_t_kernel(tc, head_res, W_merge, g_m,
         scales_of = {}
         m_of = {}
 
-        def regroup(u):
-            nb = UNITS[u]
-            raw = raw_of[u]
-            grp = grpp.tile([P, nb, D, 4], BF16, name="grp", align_bytes=64)
-            grp_of[u] = grp
-            dv = CV if u < NU - 2 else CV_LAST
-            src = raw[:].rearrange("p j (t d) -> p j t d", t=4)
+        def regroup_part(b, d0, d1):
+            raw, j = raw_of[b]
+            grp = grp_of[b]
+            src = raw[:, j, :].rearrange("p (t d) -> p t d", t=4)
+            dv = d0 + (d1 - d0) * (CV if b < NB - 3 else CV_LAST) // D
             nc.vector.tensor_copy(
-                out=grp[:, :, 0:dv, :].rearrange("p j (c i) t -> p j c t i", i=4),
-                in_=src[:, :, :, 0:dv].rearrange("p j t (c i) -> p j c t i", i=4),
+                out=grp[:, d0:dv, :].rearrange("p (c i) t -> p c t i", i=4),
+                in_=src[:, :, d0:dv].rearrange("p t (c i) -> p c t i", i=4),
             )
-            for j in range(nb):
-                nc.scalar.copy(
-                    out=grp[:, j, dv:D, :].rearrange("p (c i) t -> p c t i", i=4),
-                    in_=src[:, j, :, dv:D].rearrange("p t (c i) -> p c t i", i=4),
-                )
+            nc.scalar.copy(
+                out=grp[:, dv:d1, :].rearrange("p (c i) t -> p c t i", i=4),
+                in_=src[:, :, dv:d1].rearrange("p t (c i) -> p c t i", i=4),
+            )
 
-        def quantise(u):
-            nb = UNITS[u]
-            codes = codep.tile([P, nb * D], U32, name="codes%d" % u, align_bytes=64)
-            scales = codep.tile([P, nb * D], U8, name="scales%d" % u, align_bytes=64)
+        def regroup(b):
+            grp = grpp.tile([P, D, 4], BF16, name="grp", align_bytes=64)
+            grp_of[b] = grp
+            regroup_part(b, 0, D)
+
+        def quantise(b):
+            codes = codep.tile([P, D], U32, name="codes%d" % b, align_bytes=64)
+            scales = codep.tile([P, D], U8, name="scales%d" % b, align_bytes=64)
+            codes_of[b] = codes
+            scales_of[b] = scales
             nc.vector.quantize_mx(
                 out=codes[:].bitcast(FP8X4),
                 scales=scales[:],
-                in_=grp_of[u][:].rearrange("p j d t -> p (j d t)"),
+                in_=grp_of[b][:].rearrange("p d t -> p (d t)"),
             )
-            for j in range(nb):
-                codes_of[first_of[u] + j] = codes[:, j * D : (j + 1) * D]
-                scales_of[first_of[u] + j] = scales[:, j * D : (j + 1) * D]
 
         def product(dst, b, start, stop):
             nc.tensor.matmul_mx(
                 out=dst,
                 lhsT=w_codes[:].bitcast(FP8X4),
                 lhsT_scale=w_scales[:],
-                rhs=codes_of[b].bitcast(FP8X4),
-                rhs_scale=scales_of[b],
+                rhs=codes_of[b][:].bitcast(FP8X4),
+                rhs_scale=scales_of[b][:],
                 start=start,
                 stop=stop,
             )
@@ -149,33 +149,31 @@ def tile_block_height_reducing_filtering_pb_t_kernel(tc, head_res, W_merge, g_m,
             )
 
         sq_next = 0
-        for u in range(NU + 1):
-            if u < NU:
-                regroup(u)
-            if u == 0:
+        for s in range(NB + 1):
+            if s < NB:
+                regroup(s)
+            if s == 0:
                 nc.scalar.copy(out=w_grp[:], in_=wT_ps[:].rearrange("p t o -> p o t"))
-            if u == 1:
+            if s == 1:
                 nc.vector.quantize_mx(
                     out=w_codes[:].bitcast(FP8X4), scales=w_scales[:],
                     in_=w_grp[:].rearrange("p o t -> p (o t)"),
                 )
-            if u >= 1:
-                quantise(u - 1)
-                for j in range(UNITS[u - 1]):
-                    multiply(first_of[u - 1] + j)
-            if u == 2:
+            if s >= 1:
+                quantise(s - 1)
+                multiply(s - 1)
+            if s == 2:
                 nc.scalar.activation(
                     out=junk[:, 0:PIV], in_=m_of[0][:, 0:PIV], func=ACT.Identity, scale=-1.0 / PIV, accum_out=negc[:]
                 )
-            if u == NU - 3:
+            if s == 12:
                 with nc.allow_non_contiguous_dma(reason="one gain and one shift per partition, 128 elements each"):
                     nc.scalar.dma_start(out=g_bf[:], in_=g_m.rearrange("(o u) -> o u", u=1))
                     nc.scalar.dma_start(out=b_bf[:], in_=b_m.rearrange("(o u) -> o u", u=1))
-            if u >= 2 and u - LAGU < NU - 2:
-                while sq_next < first_of[u - LAGU] + UNITS[u - LAGU]:
-                    squares(sq_next)
-                    sq_next += 1
-
+            lag = 3 if s < LAG_SWITCH else 2
+            while sq_next <= s - lag:
+                squares(sq_next)
+                sq_next += 1
         inv = 1.0 / (NB * D)
         ssp = small.tile([P, 1], F32, name="ssp")
         bias2 = small.tile([P, 1], F32, name="bias2")
@@ -218,6 +216,7 @@ def tile_block_height_reducing_filtering_pb_t_kernel(tc, head_res, W_merge, g_m,
         )
 
         for b in range(NB):
+            i = b
             m = psum.tile([P, D], F32, name="r%d" % b, tag="m")
             product(m[:], b, True, True)
             o = outp.tile([P, D], F32, name="o%d" % b)
@@ -229,7 +228,7 @@ def tile_block_height_reducing_filtering_pb_t_kernel(tc, head_res, W_merge, g_m,
                     )
                     nc.sync.dma_start(out=out[b, :, cols], in_=o[:, cols])
                 continue
-            if b % 3 != 1:
+            if i % 3 != 1:
                 nc.scalar.activation(out=o[:], in_=m[:], func=ACT.Relu, bias=shift[:, 0:1], scale=gain[:, 0:1])
             else:
                 nc.vector.tensor_scalar(

from contextlib import ExitStack

import concourse.mybir as mybir
from concourse.masks import make_identity

FLOPS = 2 * 16 * 128 * 512 * 512

F32 = mybir.dt.float32
BF16 = mybir.dt.bfloat16
U32 = mybir.dt.uint32
U8 = mybir.dt.uint8
FP8X4 = mybir.dt.float8_e4m3fn_x4
ALU = mybir.AluOpType
ACT = mybir.ActivationFunctionType
AX = mybir.AxisListType

P = 128
NH = 4
NB = 16
D = 512
EPS = 1e-5
CHUNKS = [1] * 16
CV = 320
CV_LAST = 368
MBUFS = 7
HALF = 256
PIV = 64
MANUAL = True
LAG_SWITCH = 99


def tile_block_height_reducing_filtering_pb_t_kernel(tc, head_res, W_merge, g_m, b_m, out):
    nc = tc.nc
    with ExitStack() as ctx:
        consts = ctx.enter_context(tc.tile_pool(name="consts", bufs=1))
        rawp = ctx.enter_context(tc.tile_pool(name="rawp", bufs=1))
        grpp = ctx.enter_context(tc.tile_pool(name="grpp", bufs=4))
        codep = ctx.enter_context(tc.tile_pool(name="codep", bufs=1))
        outp = ctx.enter_context(tc.tile_pool(name="outp", bufs=1))
        small = ctx.enter_context(tc.tile_pool(name="small", bufs=1))
        psum = ctx.enter_context(tc.psum_pool(name="psum", bufs=MBUFS))
        if MANUAL:
            ctx.enter_context(tc.manual_schedule())

        w_sb = consts.tile([P, NH * P], BF16, name="w_sb")
        nc.scalar.dma_start(out=w_sb[:], in_=W_merge)
        g_bf = small.tile([P, 1], BF16, name="g_bf")
        b_bf = small.tile([P, 1], BF16, name="b_bf")

        raw_of = []
        b0 = 0
        for ci, nb in enumerate(CHUNKS):
            raw = rawp.tile([P, nb, NH * D], BF16, name="raw%d" % ci)
            for j in range(nb):
                for a in range(2):
                    nc.sync.dma_start(
                        out=raw[a:P:2, j, :].rearrange("c (b f) -> c b f", b=2),
                        in_=head_res[2 * a : 2 * a + 2, b0 + j].rearrange("b (c e) d -> c b (e d)", e=2),
                    )
            for j in range(nb):
                raw_of.append((raw, j))
            b0 += nb

        one = small.tile([P, 1], F32, name="one")
        nc.vector.memset(one[:], 1.0)
        warm = small.tile([P, 1], F32, name="warm")
        nc.scalar.activation(out=warm[:], in_=one[:], func=ACT.Abs_reciprocal_sqrt)
        ident = consts.tile([P, P], BF16, name="ident")
        make_identity(nc, ident[:])

        w_perm = consts.tile([P, 4, P], BF16, name="w_perm")
        w_src = w_sb[:].rearrange("o (a b c e) -> o b e c a", a=2, b=2, e=2)
        for b in range(2):
            nc.vector.tensor_copy(
                out=w_perm[:, 2 * b : 2 * b + 2, :].rearrange("o e (c a) -> o e c a", a=2),
                in_=w_src[:, b],
            )
        wT_ps = psum.tile([P, 4, P], BF16, name="wT_ps", tag="m")
        for t in range(4):
            nc.tensor.transpose(wT_ps[:, t, :], w_perm[:, t, :], ident[:])
        w_grp = consts.tile([P, P, 4], BF16, name="w_grp", align_bytes=64)
        w_codes = consts.tile([P, P], U32, name="w_codes", align_bytes=64)
        w_scales = consts.tile([P, P], U8, name="w_scales", align_bytes=64)

        g32 = small.tile([P, 1], F32, name="g32")
        b32 = small.tile([P, 1], F32, name="b32")

        acc = psum.tile([P, D], F32, name="acc", tag="acc", bufs=1)
        ss = small.tile([P, NB], F32, name="ss")
        junk = consts.tile([P, D], F32, name="junk")
        negc = small.tile([P, 1], F32, name="negc")

        grp_of = {}
        codes_of = {}
        scales_of = {}
        m_of = {}

        def regroup_part(b, d0, d1):
            raw, j = raw_of[b]
            grp = grp_of[b]
            src = raw[:, j, :].rearrange("p (t d) -> p t d", t=4)
            dv = d0 + (d1 - d0) * (CV if b < NB - 3 else CV_LAST) // D
            nc.vector.tensor_copy(
                out=grp[:, d0:dv, :].rearrange("p (c i) t -> p c t i", i=4),
                in_=src[:, :, d0:dv].rearrange("p t (c i) -> p c t i", i=4),
            )
            nc.scalar.copy(
                out=grp[:, dv:d1, :].rearrange("p (c i) t -> p c t i", i=4),
                in_=src[:, :, dv:d1].rearrange("p t (c i) -> p c t i", i=4),
            )

        def regroup(b):
            grp = grpp.tile([P, D, 4], BF16, name="grp", align_bytes=64)
            grp_of[b] = grp
            regroup_part(b, 0, D)

        def quantise(b):
            codes = codep.tile([P, D], U32, name="codes%d" % b, align_bytes=64)
            scales = codep.tile([P, D], U8, name="scales%d" % b, align_bytes=64)
            codes_of[b] = codes
            scales_of[b] = scales
            nc.vector.quantize_mx(
                out=codes[:].bitcast(FP8X4),
                scales=scales[:],
                in_=grp_of[b][:].rearrange("p d t -> p (d t)"),
            )

        def product(dst, b, start, stop):
            nc.tensor.matmul_mx(
                out=dst,
                lhsT=w_codes[:].bitcast(FP8X4),
                lhsT_scale=w_scales[:],
                rhs=codes_of[b][:].bitcast(FP8X4),
                rhs_scale=scales_of[b][:],
                start=start,
                stop=stop,
            )

        def multiply(b):
            product(acc[:], b, b == 0, b == NB - 1)
            m = psum.tile([P, D], F32, name="m%d" % b, tag="m")
            m_of[b] = m
            product(m[:], b, True, True)

        def squares(b):
            nc.scalar.activation(
                out=junk[:], in_=m_of[b][:], func=ACT.Square, bias=negc[:, 0:1], scale=1.0,
                accum_out=ss[:, b : b + 1],
            )

        sq_next = 0
        for s in range(NB + 1):
            if s < NB:
                regroup(s)
            if s == 0:
                nc.scalar.copy(out=w_grp[:], in_=wT_ps[:].rearrange("p t o -> p o t"))
            if s == 1:
                nc.vector.quantize_mx(
                    out=w_codes[:].bitcast(FP8X4), scales=w_scales[:],
                    in_=w_grp[:].rearrange("p o t -> p (o t)"),
                )
            if s >= 1:
                quantise(s - 1)
                multiply(s - 1)
            if s == 2:
                nc.scalar.activation(
                    out=junk[:, 0:PIV], in_=m_of[0][:, 0:PIV], func=ACT.Identity, scale=-1.0 / PIV, accum_out=negc[:]
                )
            if s == 12:
                with nc.allow_non_contiguous_dma(reason="one gain and one shift per partition, 128 elements each"):
                    nc.scalar.dma_start(out=g_bf[:], in_=g_m.rearrange("(o u) -> o u", u=1))
                    nc.scalar.dma_start(out=b_bf[:], in_=b_m.rearrange("(o u) -> o u", u=1))
            lag = 3 if s < LAG_SWITCH else 2
            while sq_next <= s - lag:
                squares(sq_next)
                sq_next += 1
        inv = 1.0 / (NB * D)
        ssp = small.tile([P, 1], F32, name="ssp")
        bias2 = small.tile([P, 1], F32, name="bias2")
        bias2b = small.tile([P, 1], F32, name="bias2b")
        s1 = small.tile([P, 1], F32, name="s1")
        dpos = small.tile([P, 1], F32, name="dpos")
        dneg = small.tile([P, 1], F32, name="dneg")
        nmean = small.tile([P, 1], F32, name="nmean")
        ngm = small.tile([P, 1], F32, name="ngm")
        bias3 = small.tile([P, 1], F32, name="bias3")
        rstd = small.tile([P, 1], F32, name="rstd")
        gain = small.tile([P, 1], F32, name="gain")
        shift = small.tile([P, 1], F32, name="shift")
        nc.vector.tensor_copy(out=g32[:], in_=g_bf[:])
        nc.vector.tensor_copy(out=b32[:], in_=b_bf[:])
        nc.vector.reduce_sum(out=ssp[:], in_=ss[:, 0 : NB - 2], axis=AX.X)
        nc.vector.tensor_scalar(out=bias2[:], in0=ssp[:], scalar1=inv, scalar2=EPS, op0=ALU.mult, op1=ALU.add)
        while sq_next < NB:
            squares(sq_next)
            sq_next += 1
        nc.vector.reduce_sum(out=s1[:], in_=acc[:], axis=AX.X)
        nc.vector.tensor_scalar(out=dpos[:], in0=s1[:], scalar1=inv, scalar2=negc[:, 0:1], op0=ALU.mult, op1=ALU.add)
        nc.vector.tensor_scalar(
            out=dneg[:], in0=s1[:], scalar1=-inv, scalar2=negc[:, 0:1], op0=ALU.mult, op1=ALU.subtract
        )
        nc.vector.scalar_tensor_tensor(
            out=bias2b[:], in0=ss[:, NB - 2 : NB - 1], scalar=inv, in1=bias2[:], op0=ALU.mult, op1=ALU.add
        )
        nc.vector.scalar_tensor_tensor(
            out=bias3[:], in0=dpos[:], scalar=dneg[:, 0:1], in1=bias2b[:], op0=ALU.mult, op1=ALU.add
        )
        nc.scalar.activation(
            out=rstd[:], in_=ss[:, NB - 1 : NB], func=ACT.Abs_reciprocal_sqrt, bias=bias3[:, 0:1], scale=inv
        )
        nc.vector.tensor_scalar(out=nmean[:], in0=s1[:], scalar1=-inv, scalar2=None, op0=ALU.mult)
        nc.vector.tensor_tensor(out=ngm[:], in0=nmean[:], in1=g32[:], op=ALU.mult)
        nc.vector.tensor_tensor(out=gain[:], in0=g32[:], in1=rstd[:], op=ALU.mult)
        nc.vector.scalar_tensor_tensor(
            out=shift[:], in0=ngm[:], scalar=rstd[:, 0:1], in1=b32[:], op0=ALU.mult, op1=ALU.add
        )

        for b in range(NB):
            i = b
            m = psum.tile([P, D], F32, name="r%d" % b, tag="m")
            product(m[:], b, True, True)
            o = outp.tile([P, D], F32, name="o%d" % b)
            if b == 0:
                for h in range(2):
                    cols = slice(h * HALF, (h + 1) * HALF)
                    nc.scalar.activation(
                        out=o[:, cols], in_=m[:, cols], func=ACT.Relu, bias=shift[:, 0:1], scale=gain[:, 0:1]
                    )
                    nc.sync.dma_start(out=out[b, :, cols], in_=o[:, cols])
                continue
            if i % 3 != 1:
                nc.scalar.activation(out=o[:], in_=m[:], func=ACT.Relu, bias=shift[:, 0:1], scale=gain[:, 0:1])
            else:
                nc.vector.tensor_scalar(
                    out=o[:], in0=m[:], scalar1=gain[:, 0:1], scalar2=shift[:, 0:1], op0=ALU.mult, op1=ALU.add
                )
                nc.vector.tensor_scalar_max(out=o[:], in0=o[:], scalar1=0.0)
            nc.sync.dma_start(out=out[b], in_=o[:])
